import numpy as np
import ml_dtypes


def mxq(x, axis, fmt="e4m3"):
    dtype, down = {"e4m3": (ml_dtypes.float8_e4m3fn, 7), "e5m2": (ml_dtypes.float8_e5m2, 14)}[fmt]
    v = np.moveaxis(np.asarray(x, np.float32).astype(ml_dtypes.bfloat16).astype(np.float64), axis, -1)
    blocks = v.reshape(v.shape[:-1] + (-1, 32))
    amax = np.abs(blocks).max(-1, keepdims=True)
    byte = np.maximum(np.where(amax > 0, np.frexp(amax)[1] - 1 + 127, 0) - down, 1)
    scale = np.exp2(byte - 127.0)
    codes = (blocks / scale).astype(np.float32).astype(dtype).astype(np.float64)
    return np.moveaxis((codes * scale).reshape(v.shape), -1, axis)


WIDE = False


def mx_kscale(k):
    if not WIDE:
        return np.ones(k)
    levels = np.array([30, -30])
    if k % 512:
        return np.exp2(np.random.permutation(np.resize(levels, k // 32))).repeat(32)
    a = np.empty((k // 512, 16))
    for p in range(k // 512):
        a[p, :8] = np.random.permutation(np.resize(levels, 8))
        for g in range(8):
            far = levels[np.abs(levels - a[p, g]) >= 10]
            a[p, g + 8] = far[np.random.randint(len(far))]
    return np.exp2(a.ravel()).repeat(32)


BF16 = ml_dtypes.bfloat16


def bf(x):
    return np.asarray(x, np.float32).astype(BF16)


def f64(x):
    return np.asarray(x).astype(np.float64)


E2M1 = np.array([0.0, 0.5, 1.0, 1.5, 2.0, 3.0, 4.0, 6.0, -0.0, -0.5, -1.0, -1.5, -2.0, -3.0, -4.0, -6.0])


def pack_weight(w, fmt):
    k, n = w.shape
    w = f64(bf(w)).reshape(k // 32, 32, n)
    amax = np.abs(w).max(1)
    if fmt == "e4m3":
        byte = np.frexp(amax)[1] - 1 + 127 - 7
    else:
        mant, ex = np.frexp(amax / 6.0)
        byte = np.where(mant > 0.5, ex, ex - 1) + 127
    byte = np.clip(np.where(amax > 0, byte, 1), 1, 254)
    scaled = (w * np.exp2(127.0 - byte)[:, None, :]).reshape(k, n).astype(np.float32)
    by_word = np.ascontiguousarray(scaled.reshape(k // 512, 128, 4, n).transpose(0, 1, 3, 2))
    if fmt == "e4m3":
        words = by_word.astype(ml_dtypes.float8_e4m3fn).view(np.uint8)
    else:
        c = by_word.astype(ml_dtypes.float4_e2m1fn).view(np.uint8) & 0xF
        words = c[..., 0::2] | (c[..., 1::2] << 4)
    return np.ascontiguousarray(words), np.ascontiguousarray(byte.astype(np.uint8).reshape(k // 512, 16, n))


def unpack_weight(words, scales, fmt):
    g, p, n, _ = words.shape
    if fmt == "e4m3":
        vals = np.ascontiguousarray(words).view(ml_dtypes.float8_e4m3fn).astype(np.float64)
    else:
        nib = np.empty((g, p, n, 4), np.uint8)
        nib[..., 0::2] = words & 0xF
        nib[..., 1::2] = words >> 4
        vals = E2M1[nib]
    vals = vals * np.repeat(np.exp2(scales.astype(np.float64) - 127.0), 8, axis=1)[..., None]
    return vals.transpose(0, 1, 3, 2).reshape(g * 512, n)

def pack4(w):
    words, scales = pack_weight(w, "e2m1")
    return words.reshape(words.shape[0], 128, -1), scales


def unpack4(words, scales):
    return unpack_weight(words.reshape(words.shape[0], 128, -1, 2), scales, "e2m1")


LQ, LK, D, H, DK, DV = 1024, 1024, 2048, 4, 128, 128
HV = H * DV
LN_EPS = 1e-5


def setup_inputs():
    s = mx_kscale(HV)
    attn_out = bf(np.random.standard_normal((H, LQ, DV)) * 0.7 * s.reshape(H, DV)[:, None, :])
    residual = bf(np.random.standard_normal((LQ, D)))
    words, scales = pack4(np.random.standard_normal((HV, D)) / np.sqrt(HV) / s[:, None])
    proj_b = bf(np.random.standard_normal(D) * 0.3)
    ln_g = bf(1.0 + 0.1 * np.random.standard_normal(D))
    ln_b = bf(0.1 * np.random.standard_normal(D))
    return {"attn_out": attn_out,
            "residual": residual,
            "proj_w_words": words,
            "proj_w_scales": scales,
            "proj_b": proj_b,
            "ln_g": ln_g,
            "ln_b": ln_b}


def reference(attn_out, residual, proj_w_words, proj_w_scales, proj_b, ln_g, ln_b):
    x = f64(attn_out).transpose(1, 0, 2).reshape(LQ, HV)
    y = (mxq(x, 1, "e5m2") @ unpack4(proj_w_words, proj_w_scales)) + f64(proj_b) + f64(residual)
    mu = y.mean(-1, keepdims=True)
    var = ((y - mu) ** 2).mean(-1, keepdims=True)
    return (y - mu) / np.sqrt(var + LN_EPS) * f64(ln_g) + f64(ln_b)

@@ -1,0 +1,379 @@
+from contextlib import ExitStack
+
+import concourse.mybir as mybir
+from concourse.masks import make_identity
+
+LQ, D, H, DV = 1024, 2048, 4, 128
+HV = H * DV
+LN_EPS = 1e-5
+FLOPS = 2 * LQ * HV * D
+
+F32 = mybir.dt.float32
+BF16 = mybir.dt.bfloat16
+I32 = mybir.dt.int32
+U32 = mybir.dt.uint32
+U8 = mybir.dt.uint8
+E5M2X4 = mybir.dt.float8_e5m2_x4
+E2M1X4 = mybir.dt.float4_e2m1fn_x4
+ACT = mybir.ActivationFunctionType
+ALU = mybir.AluOpType
+
+P = 128
+PACK = 4
+BLOCK = 512
+BLOCKS = D // BLOCK
+SUBS = BLOCK // P
+TILES = LQ // P
+BANK_BF16 = 1024
+HALF = D // 2
+TURNED = 2
+V_MAX = 1536
+G_MIN = 1024
+V_COLS = [1216,1216,1216,1216,1216,1216,1408,1536]
+LAG = 2
+STORE_LAG = 2
+
+
+def tile_multiheadattention_pb_kernel(
+    tc, attn_out, residual, proj_w_words, proj_w_scales, proj_b, ln_g, ln_b, out
+):
+    nc = tc.nc
+    turned = list(range(TURNED))
+    direct = list(range(TURNED, BLOCKS))
+    tail = V_MAX - BANK_BF16
+
+    with ExitStack() as ctx:
+        keep = ctx.enter_context(tc.tile_pool(name="keep", bufs=1))
+        work = ctx.enter_context(tc.tile_pool(name="work", bufs=3))
+        stat = ctx.enter_context(tc.tile_pool(name="stat", bufs=4))
+        fixed = ctx.enter_context(tc.psum_pool(name="fixed", bufs=1))
+        banks = ctx.enter_context(tc.psum_pool(name="banks", bufs=5))
+        ctx.enter_context(tc.manual_schedule())
+
+        bias_rows = keep.tile([P, BLOCK], BF16)
+        norm_rows = keep.tile([P, BLOCK], BF16)
+        w_scales = keep.tile([P, D], U8, align_bytes=64)
+        w_words = keep.tile([P, 2 * D], U8, align_bytes=64)
+        ident = keep.tile([P, P], F32)
+        ident_bf = keep.tile([P, P], BF16)
+        nc.vector.memset(bias_rows[:], 0.0)
+        nc.vector.memset(w_scales[:].bitcast(I32), 0)
+        nc.vector.memset(norm_rows[:], 0.0)
+        make_identity(nc, ident[:])
+        make_identity(nc, ident_bf[:])
+
+        x_rows = []
+        res = []
+        for i in range(TILES):
+            x_rows.append(keep.tile([P, HV], BF16, name="x_rows%d" % i))
+            res.append(keep.tile([P, D], BF16, name="res%d" % i))
+
+        def load_x(i):
+            nc.sync.dma_start(
+                out=x_rows[i][:].rearrange("p (h j) -> p h j", h=H),
+                in_=attn_out[:, i * P : (i + 1) * P, :].rearrange("h p j -> p h j"),
+            )
+
+        def load_res(i):
+            nc.sync.dma_start(out=res[i][:], in_=residual[i * P : (i + 1) * P, :])
+
+        gain_g = keep.tile([P, D - G_MIN], BF16)
+        beta_g = keep.tile([P, D - G_MIN], BF16)
+        load_x(0)
+        nc.sync.dma_start(out=bias_rows[0:BLOCKS, :], in_=proj_b.rearrange("(r n) -> r n", n=BLOCK))
+        load_x(1)
+        for q in range(4):
+            nc.sync.dma_start(
+                out=w_scales[32 * q : 32 * q + 4, :].bitcast(I32),
+                in_=proj_w_scales[0, 4 * q : 4 * q + 4, :].bitcast(I32),
+            )
+        nc.sync.dma_start(out=w_words[:].bitcast(I32), in_=proj_w_words[0].bitcast(I32))
+        nc.gpsimd.dma_start(out=norm_rows[0:BLOCKS, :], in_=ln_g.rearrange("(r n) -> r n", n=BLOCK))
+        nc.gpsimd.dma_start(out=norm_rows[BLOCKS : 2 * BLOCKS, :], in_=ln_b.rearrange("(r n) -> r n", n=BLOCK))
+        for i in range(TILES):
+            load_res(i)
+            for k in range(4 * i + 2, min(4 * i + 6, TILES)):
+                load_x(k)
+            if i == 4:
+                nc.sync.dma_start(out=gain_g[:], in_=ln_g[G_MIN:D].partition_broadcast(P))
+                nc.sync.dma_start(out=beta_g[:], in_=ln_b[G_MIN:D].partition_broadcast(P))
+
+        x_codes = {}
+        x_scales = {}
+
+        def turn_x(tiles, grouped, first, bank):
+            n = len(tiles)
+            xt = fixed.tile([P, n, 2, P], F32, name="xt", tag=bank)
+            for t, i in enumerate(tiles):
+                words = x_rows[i][:].bitcast(F32)
+                for u in range(2):
+                    nc.tensor.transpose(xt[:, t, u, :], words[:, u : HV // 2 : 2], ident[:])
+            nc.scalar.copy(
+                out=grouped[:, first * HV : (first + n) * HV].bitcast(F32).rearrange("p (t r u) -> p t r u", t=n, u=2),
+                in_=xt[:].rearrange("p t u r -> p t r u"),
+            )
+
+        def quantize_x(tiles, grouped):
+            n = len(tiles)
+            codes = keep.tile([P, n * P], U32, name="codes%d" % tiles[0], align_bytes=64)
+            scales = keep.tile([P, n * P], U8, name="scales%d" % tiles[0], align_bytes=64)
+            nc.vector.quantize_mx(out=codes[:].bitcast(E5M2X4), scales=scales[:], in_=grouped[:])
+            for t, i in enumerate(tiles):
+                x_codes[i] = codes[:, t * P : (t + 1) * P].bitcast(E5M2X4)
+                x_scales[i] = scales[:, t * P : (t + 1) * P]
+
+        def spread(dst, rows, first_row, c0, c1):
+            c = c0
+            while c < c1:
+                r = c // BLOCK
+                end = min(c1, (r + 1) * BLOCK, c + BLOCK - (c - c0) % BLOCK)
+                nc.tensor.matmul(
+                    out=dst[:, c - c0 : end - c0],
+                    lhsT=ident_bf[:, first_row + r : first_row + r + 1].to_broadcast([P, P]),
+                    rhs=rows[:, c - r * BLOCK : end - r * BLOCK],
+                    start=True,
+                    stop=True,
+                )
+                c = end
+
+        res_bias = {}
+
+        def add_bias(i, half, engine, bias):
+            res_bias[i, half] = keep.tile([P, HALF], F32, name="res_bias%d_%d" % (i, half))
+            engine.tensor_tensor(
+                out=res_bias[i, half][:], in0=res[i][:, half * HALF : (half + 1) * HALF], in1=bias, op=ALU.add
+            )
+
+        proj = {}
+        turned_sb = {}
+
+        def project_turned(i, j):
+            acc = banks.tile([P, BLOCK], F32, name="acc", tag="bank")
+            for s in range(SUBS):
+                c0 = j * BLOCK + s * P
+                nc.tensor.matmul_mx(
+                    out=acc[:, s * P : (s + 1) * P],
+                    lhsT=w_words[:, 2 * c0 : 2 * (c0 + P)].bitcast(E2M1X4),
+                    lhsT_scale=w_scales[:, c0 : c0 + P],
+                    rhs=x_codes[i],
+                    rhs_scale=x_scales[i],
+                    start=True,
+                    stop=True,
+                )
+            proj[i, j] = acc
+
+        def bias_turned(i, j):
+            sb = work.tile([P, BLOCK], F32, name="turned%d" % j)
+            turned_sb[i, j] = sb
+            for s in range(SUBS):
+                nc.scalar.activation(
+                    out=sb[:, s * P : (s + 1) * P],
+                    in_=proj[i, j][:, s * P : (s + 1) * P],
+                    func=ACT.Identity,
+                    bias=bias_cols[:, s, j : j + 1],
+                )
+
+        def turn_back(i, j):
+            for s in range(SUBS):
+                nc.tensor.transpose(
+                    proj[i, j][:, s * P : (s + 1) * P], turned_sb[i, j][:, s * P : (s + 1) * P], ident[:]
+                )
+
+        def project_direct(i, j):
+            acc = banks.tile([P, BLOCK], F32, name="acc", tag="bank")
+            nc.tensor.matmul_mx(
+                out=acc[:],
+                lhsT=x_codes[i],
+                lhsT_scale=x_scales[i],
+                rhs=w_words[:, 2 * j * BLOCK : 2 * (j + 1) * BLOCK].bitcast(E2M1X4),
+                rhs_scale=w_scales[:, j * BLOCK : (j + 1) * BLOCK],
+                start=True,
+                stop=True,
+            )
+            proj[i, j] = acc
+
+        y = {}
+        sums = {}
+        neg_mean = {}
+        sum_sq = {}
+        std = {}
+        rstd = {}
+        shift = {}
+        out_g = {}
+
+        def add_residual(i, j):
+            if i not in y:
+                y[i] = work.tile([P, D], F32, name="y", bufs=4)
+                sums[i] = stat.tile([P, BLOCKS], F32, name="sums")
+            cols = slice(j * BLOCK, (j + 1) * BLOCK)
+            half, at = divmod(j * BLOCK, HALF)
+            other = res_bias[i, half][:, at : at + BLOCK] if (i, half) in res_bias else res[i][:, cols]
+            nc.vector.scalar_tensor_tensor(
+                out=y[i][:, cols],
+                in0=proj[i, j][:],
+                scalar=1.0,
+                in1=other,
+                op0=ALU.mult,
+                op1=ALU.add,
+                accum_out=sums[i][:, j : j + 1],
+            )
+
+        def mean_of(i):
+            scaled = stat.tile([P, BLOCKS], F32, name="scaled")
+            neg_mean[i] = stat.tile([P, 1], F32, name="neg_mean")
+            nc.scalar.activation(
+                out=scaled[:], in_=sums[i][:], func=ACT.Identity, scale=-1.0 / D, accum_out=neg_mean[i][:]
+            )
+
+        def squares_of(i):
+            squares = keep.tile([P, D], BF16, name="squares")
+            sum_sq[i] = stat.tile([P, 1], F32, name="sum_sq")
+            nc.scalar.activation(
+                out=squares[:], in_=y[i][:], func=ACT.Square, bias=neg_mean[i][:], accum_out=sum_sq[i][:]
+            )
+
+        def std_of(i):
+            std[i] = stat.tile([P, 1], F32, name="std")
+            nc.scalar.activation(out=std[i][:], in_=sum_sq[i][:], func=ACT.Sqrt, scale=1.0 / D, bias=LN_EPS)
+
+        def rstd_of(i):
+            rstd[i] = stat.tile([P, 1], F32, name="rstd")
+            nc.vector.reciprocal(out=rstd[i][:], in_=std[i][:])
+
+        def shift_of(i):
+            shift[i] = stat.tile([P, 1], F32, name="shift")
+            nc.scalar.activation(out=shift[i][:], in_=neg_mean[i][:], func=ACT.Identity, scale=rstd[i][:])
+
+        def normalise_g(i):
+            out_g[i] = work.tile([P, D - V_COLS[i]], F32, name="out_g", bufs=5)
+            nc.scalar.activation(
+                out=out_g[i][:], in_=y[i][:, V_COLS[i] : D], func=ACT.Identity, scale=rstd[i][:], bias=shift[i][:]
+            )
+
+        def finish_g(i):
+            cols = slice(V_COLS[i] - G_MIN, D - G_MIN)
+            nc.gpsimd.tensor_tensor(out=out_g[i][:], in0=out_g[i][:], in1=gain_g[:, cols], op=ALU.mult)
+            nc.gpsimd.tensor_tensor(out=out_g[i][:], in0=out_g[i][:], in1=beta_g[:, cols], op=ALU.add)
+
+        def store_g(i):
+            nc.sync.dma_start(out=out[i * P : (i + 1) * P, V_COLS[i] : D], in_=out_g[i][:])
+
+        def finish_v(i, between):
+            out_v = work.tile([P, V_COLS[i]], F32, name="out_v")
+            parts = [(slice(0, BANK_BF16), gain_head[:], beta_head[:])]
+            rest = V_COLS[i] - BANK_BF16
+            if rest:
+                parts.append((slice(BANK_BF16, V_COLS[i]), both_tail[:, 0:rest], both_tail[:, tail : tail + rest]))
+            for cols, gain, beta in parts:
+                nc.vector.scalar_tensor_tensor(
+                    out=out_v[:, cols], in0=y[i][:, cols], scalar=neg_mean[i][:], in1=gain, op0=ALU.add, op1=ALU.mult
+                )
+            if between is not None:
+                rstd_of(between)
+            for cols, gain, beta in parts:
+                nc.vector.scalar_tensor_tensor(
+                    out=out_v[:, cols], in0=out_v[:, cols], scalar=rstd[i][:], in1=beta, op0=ALU.mult, op1=ALU.add
+                )
+                nc.sync.dma_start(out=out[i * P : (i + 1) * P, cols], in_=out_v[:, cols])
+
+        first, second = turned
+        grouped01 = keep.tile([P, 2 * HV], BF16, align_bytes=64)
+        grouped23 = keep.tile([P, 2 * HV], BF16, align_bytes=64)
+        grouped47 = keep.tile([P, 4 * HV], BF16, align_bytes=64)
+        turn_x([0, 1], grouped01, 0, "f0")
+        quantize_x([0, 1], grouped01)
+        bias_high = fixed.tile([P, HALF], BF16, name="bias_high", tag="f1")
+        spread(bias_high, bias_rows, 0, HALF, D)
+        bias_wide = keep.tile([P, HALF], BF16)
+        nc.scalar.copy(out=bias_wide[:], in_=bias_high[:])
+        for j in direct:
+            project_direct(0, j)
+        bias_low = fixed.tile([P, HALF], BF16, name="bias_low", tag="f2")
+        spread(bias_low, bias_rows, 0, 0, HALF)
+        for j in turned:
+            project_direct(0, j)
+        bias_t = banks.tile([P, SUBS, P], BF16, name="bias_t", tag="bank")
+        for s in range(SUBS):
+            nc.tensor.transpose(bias_t[:, s, :], bias_rows[:, s * P : (s + 1) * P], ident_bf[:])
+        bias_cols = keep.tile([P, SUBS, BLOCKS], F32)
+        nc.scalar.copy(out=bias_cols[:], in_=bias_t[:, :, 0:BLOCKS])
+        turn_x([2, 3], grouped23, 0, "f0")
+
+        add_bias(0, 1, nc.vector, bias_high[:])
+        for j in direct:
+            add_residual(0, j)
+        add_bias(0, 0, nc.vector, bias_low[:])
+        quantize_x([2, 3], grouped23)
+        for i in range(1, TILES):
+            add_bias(i, 1, nc.gpsimd, bias_wide[:])
+        for j in turned:
+            add_residual(0, j)
+        add_bias(1, 0, nc.vector, bias_low[:])
+
+        for j in turned:
+            project_direct(1, j)
+        turn_x([4, 5], grouped47, 0, "f1")
+        project_turned(2, first)
+        bias_turned(2, first)
+        for j in direct:
+            project_direct(1, j)
+        mean_of(0)
+        turn_x([6, 7], grouped47, 2, "f0")
+        squares_of(0)
+        turn_back(2, first)
+        for j in turned + direct:
+            add_residual(1, j)
+        project_turned(2, second)
+        bias_turned(2, second)
+        std_of(0)
+        for j in direct:
+            project_direct(2, j)
+        gain_head = fixed.tile([P, BANK_BF16], BF16, name="gain_head", tag="f1")
+        spread(gain_head, norm_rows, 0, 0, BANK_BF16)
+        turn_back(2, second)
+        project_turned(3, first)
+        both_tail = fixed.tile([P, 2 * tail], BF16, name="both_tail", tag="f0")
+        spread(both_tail[:, 0:tail], norm_rows, 0, BANK_BF16, V_MAX)
+        beta_head = fixed.tile([P, BANK_BF16], BF16, name="beta_head", tag="f2")
+        spread(beta_head, norm_rows, BLOCKS, 0, BANK_BF16)
+        spread(both_tail[:, tail : 2 * tail], norm_rows, BLOCKS, BANK_BF16, V_MAX)
+
+        for i in range(LAG, TILES + LAG):
+            if i < TILES:
+                add_residual(i, direct[0])
+            if LAG < i <= TILES:
+                rstd_of(i - LAG)
+            if i < TILES:
+                add_residual(i, direct[1])
+                for j in turned:
+                    add_residual(i, j)
+            if i == LAG:
+                quantize_x([4, 5, 6, 7], grouped47)
+            if i - 1 < TILES:
+                mean_of(i - 1)
+            if i + 1 < TILES:
+                bias_turned(i + 1, first)
+                project_turned(i + 1, second)
+                project_direct(i + 1, direct[0])
+                project_direct(i + 1, direct[1])
+                turn_back(i + 1, first)
+            if i + 2 < TILES:
+                project_turned(i + 2, first)
+            if i - 1 < TILES:
+                squares_of(i - 1)
+            if i == LAG:
+                finish_v(0, 0)
+            shift_of(i - LAG)
+            if i - 1 < TILES:
+                std_of(i - 1)
+            normalise_g(i - LAG)
+            if i + 1 < TILES:
+                bias_turned(i + 1, second)
+                turn_back(i + 1, second)
+            if i > LAG:
+                finish_v(i - LAG, TILES - 1 if i == TILES else None)
+            finish_g(i - LAG)
+            if i >= LAG + STORE_LAG:
+                store_g(i - LAG - STORE_LAG)
+        for i in range(TILES - STORE_LAG, TILES):
+            store_g(i)

@@ -29,9 +29,9 @@ HALF = D // 2
 TURNED = 2
 V_MAX = 1536
 G_MIN = 1024
-V_COLS = [1216,1216,1216,1216,1216,1216,1408,1536]
+V_COLS = [1376,1376,1376,1376,1376,1376,1376,1376]
 LAG = 2
-STORE_LAG = 2
+STORE_LAG = 0
 
 
 def tile_multiheadattention_pb_kernel(
@@ -80,23 +80,32 @@ def tile_multiheadattention_pb_kernel(
         gain_g = keep.tile([P, D - G_MIN], BF16)
         beta_g = keep.tile([P, D - G_MIN], BF16)
         load_x(0)
-        nc.sync.dma_start(out=bias_rows[0:BLOCKS, :], in_=proj_b.rearrange("(r n) -> r n", n=BLOCK))
         load_x(1)
+        load_x(2)
+        load_x(3)
+        nc.sync.dma_start(out=bias_rows[0:BLOCKS, :], in_=proj_b.rearrange("(r n) -> r n", n=BLOCK))
         for q in range(4):
             nc.sync.dma_start(
                 out=w_scales[32 * q : 32 * q + 4, :].bitcast(I32),
                 in_=proj_w_scales[0, 4 * q : 4 * q + 4, :].bitcast(I32),
             )
         nc.sync.dma_start(out=w_words[:].bitcast(I32), in_=proj_w_words[0].bitcast(I32))
-        nc.gpsimd.dma_start(out=norm_rows[0:BLOCKS, :], in_=ln_g.rearrange("(r n) -> r n", n=BLOCK))
-        nc.gpsimd.dma_start(out=norm_rows[BLOCKS : 2 * BLOCKS, :], in_=ln_b.rearrange("(r n) -> r n", n=BLOCK))
-        for i in range(TILES):
-            load_res(i)
-            for k in range(4 * i + 2, min(4 * i + 6, TILES)):
-                load_x(k)
-            if i == 4:
-                nc.sync.dma_start(out=gain_g[:], in_=ln_g[G_MIN:D].partition_broadcast(P))
-                nc.sync.dma_start(out=beta_g[:], in_=ln_b[G_MIN:D].partition_broadcast(P))
+        load_res(0)
+        load_res(1)
+        load_x(4)
+        load_x(5)
+        load_res(2)
+        load_x(6)
+        load_x(7)
+        nc.sync.dma_start(out=norm_rows[0:BLOCKS, :], in_=ln_g.rearrange("(r n) -> r n", n=BLOCK))
+        nc.sync.dma_start(out=norm_rows[BLOCKS : 2 * BLOCKS, :], in_=ln_b.rearrange("(r n) -> r n", n=BLOCK))
+        load_res(3)
+        load_res(4)
+        nc.sync.dma_start(out=gain_g[:], in_=ln_g[G_MIN:D].partition_broadcast(P))
+        nc.sync.dma_start(out=beta_g[:], in_=ln_b[G_MIN:D].partition_broadcast(P))
+        load_res(5)
+        load_res(6)
+        load_res(7)
 
         x_codes = {}
         x_scales = {}
@@ -139,7 +148,7 @@ def tile_multiheadattention_pb_kernel(
         res_bias = {}
 
         def add_bias(i, half, engine, bias):
-            res_bias[i, half] = keep.tile([P, HALF], F32, name="res_bias%d_%d" % (i, half))
+            res_bias[i, half] = keep.tile([P, HALF], F32, name="res_bias", tag="res_bias%d" % i, align_bytes=64)
             engine.tensor_tensor(
                 out=res_bias[i, half][:], in0=res[i][:, half * HALF : (half + 1) * HALF], in1=bias, op=ALU.add
             )
@@ -162,7 +171,7 @@ def tile_multiheadattention_pb_kernel(
                 )
             proj[i, j] = acc
 
-        def bias_turned(i, j):
+        def bias_turned(i, j, between=()):
             sb = work.tile([P, BLOCK], F32, name="turned%d" % j)
             turned_sb[i, j] = sb
             for s in range(SUBS):
@@ -172,6 +181,8 @@ def tile_multiheadattention_pb_kernel(
                     func=ACT.Identity,
                     bias=bias_cols[:, s, j : j + 1],
                 )
+                if s < len(between):
+                    between[s]()
 
         def turn_back(i, j):
             for s in range(SUBS):
@@ -196,7 +207,6 @@ def tile_multiheadattention_pb_kernel(
         sums = {}
         neg_mean = {}
         sum_sq = {}
-        std = {}
         rstd = {}
         shift = {}
         out_g = {}
@@ -232,13 +242,11 @@ def tile_multiheadattention_pb_kernel(
                 out=squares[:], in_=y[i][:], func=ACT.Square, bias=neg_mean[i][:], accum_out=sum_sq[i][:]
             )
 
-        def std_of(i):
-            std[i] = stat.tile([P, 1], F32, name="std")
-            nc.scalar.activation(out=std[i][:], in_=sum_sq[i][:], func=ACT.Sqrt, scale=1.0 / D, bias=LN_EPS)
-
         def rstd_of(i):
             rstd[i] = stat.tile([P, 1], F32, name="rstd")
-            nc.vector.reciprocal(out=rstd[i][:], in_=std[i][:])
+            nc.scalar.activation(
+                out=rstd[i][:], in_=sum_sq[i][:], func=ACT.Abs_reciprocal_sqrt, scale=1.0 / D, bias=LN_EPS
+            )
 
         def shift_of(i):
             shift[i] = stat.tile([P, 1], F32, name="shift")
@@ -258,7 +266,7 @@ def tile_multiheadattention_pb_kernel(
         def store_g(i):
             nc.sync.dma_start(out=out[i * P : (i + 1) * P, V_COLS[i] : D], in_=out_g[i][:])
 
-        def finish_v(i, between):
+        def finish_v(i):
             out_v = work.tile([P, V_COLS[i]], F32, name="out_v")
             parts = [(slice(0, BANK_BF16), gain_head[:], beta_head[:])]
             rest = V_COLS[i] - BANK_BF16
@@ -268,8 +276,6 @@ def tile_multiheadattention_pb_kernel(
                 nc.vector.scalar_tensor_tensor(
                     out=out_v[:, cols], in0=y[i][:, cols], scalar=neg_mean[i][:], in1=gain, op0=ALU.add, op1=ALU.mult
                 )
-            if between is not None:
-                rstd_of(between)
             for cols, gain, beta in parts:
                 nc.vector.scalar_tensor_tensor(
                     out=out_v[:, cols], in0=out_v[:, cols], scalar=rstd[i][:], in1=beta, op0=ALU.mult, op1=ALU.add
@@ -277,102 +283,87 @@ def tile_multiheadattention_pb_kernel(
                 nc.sync.dma_start(out=out[i * P : (i + 1) * P, cols], in_=out_v[:, cols])
 
         first, second = turned
-        grouped01 = keep.tile([P, 2 * HV], BF16, align_bytes=64)
-        grouped23 = keep.tile([P, 2 * HV], BF16, align_bytes=64)
-        grouped47 = keep.tile([P, 4 * HV], BF16, align_bytes=64)
-        turn_x([0, 1], grouped01, 0, "f0")
-        quantize_x([0, 1], grouped01)
-        bias_high = fixed.tile([P, HALF], BF16, name="bias_high", tag="f1")
-        spread(bias_high, bias_rows, 0, HALF, D)
-        bias_wide = keep.tile([P, HALF], BF16)
-        nc.scalar.copy(out=bias_wide[:], in_=bias_high[:])
-        for j in direct:
-            project_direct(0, j)
-        bias_low = fixed.tile([P, HALF], BF16, name="bias_low", tag="f2")
-        spread(bias_low, bias_rows, 0, 0, HALF)
-        for j in turned:
-            project_direct(0, j)
+        grouped03 = keep.tile([P, 4 * HV], BF16, align_bytes=64)
+        grouped47 = keep.tile([P, 4 * HV], BF16, name="grouped47", tag="res_bias3", align_bytes=64)
+        turn_x([0, 1], grouped03, 0, "f0")
+        turn_x([2, 3], grouped03, 2, "f1")
+        quantize_x([0, 1, 2, 3], grouped03)
         bias_t = banks.tile([P, SUBS, P], BF16, name="bias_t", tag="bank")
         for s in range(SUBS):
             nc.tensor.transpose(bias_t[:, s, :], bias_rows[:, s * P : (s + 1) * P], ident_bf[:])
         bias_cols = keep.tile([P, SUBS, BLOCKS], F32)
         nc.scalar.copy(out=bias_cols[:], in_=bias_t[:, :, 0:BLOCKS])
-        turn_x([2, 3], grouped23, 0, "f0")
-
+        bias_high = fixed.tile([P, HALF], BF16, name="bias_high", tag="f2")
+        spread(bias_high, bias_rows, 0, HALF, D)
+        bias_wide = keep.tile([P, HALF], BF16)
+        nc.scalar.copy(out=bias_wide[:], in_=bias_high[:])
         add_bias(0, 1, nc.vector, bias_high[:])
-        for j in direct:
-            add_residual(0, j)
-        add_bias(0, 0, nc.vector, bias_low[:])
-        quantize_x([2, 3], grouped23)
-        for i in range(1, TILES):
-            add_bias(i, 1, nc.gpsimd, bias_wide[:])
-        for j in turned:
-            add_residual(0, j)
-        add_bias(1, 0, nc.vector, bias_low[:])
+        add_bias(1, 1, nc.gpsimd, bias_wide[:])
 
         for j in turned:
+            project_turned(0, j)
+            bias_turned(0, j)
+        for j in direct:
+            project_direct(0, j)
+        project_turned(1, first)
+        bias_turned(1, first)
+        for j in turned:
+            turn_back(0, j)
+        for j in direct + turned:
+            add_residual(0, j)
+        project_turned(1, second)
+        bias_turned(1, second)
+        turn_x([4, 5], grouped47, 0, "f0")
+        for j in direct:
             project_direct(1, j)
-        turn_x([4, 5], grouped47, 0, "f1")
+        turn_back(1, first)
+        turn_x([6, 7], grouped47, 2, "f1")
+        turn_back(1, second)
+        add_bias(2, 1, nc.gpsimd, bias_wide[:])
         project_turned(2, first)
-        bias_turned(2, first)
-        for j in direct:
-            project_direct(1, j)
         mean_of(0)
-        turn_x([6, 7], grouped47, 2, "f0")
-        squares_of(0)
-        turn_back(2, first)
-        for j in turned + direct:
-            add_residual(1, j)
-        project_turned(2, second)
-        bias_turned(2, second)
-        std_of(0)
-        for j in direct:
-            project_direct(2, j)
-        gain_head = fixed.tile([P, BANK_BF16], BF16, name="gain_head", tag="f1")
-        spread(gain_head, norm_rows, 0, 0, BANK_BF16)
-        turn_back(2, second)
-        project_turned(3, first)
-        both_tail = fixed.tile([P, 2 * tail], BF16, name="both_tail", tag="f0")
-        spread(both_tail[:, 0:tail], norm_rows, 0, BANK_BF16, V_MAX)
-        beta_head = fixed.tile([P, BANK_BF16], BF16, name="beta_head", tag="f2")
-        spread(beta_head, norm_rows, BLOCKS, 0, BANK_BF16)
-        spread(both_tail[:, tail : 2 * tail], norm_rows, BLOCKS, BANK_BF16, V_MAX)
+        bias_turned(2, first)
 
-        for i in range(LAG, TILES + LAG):
+        for i in range(1, TILES + LAG):
             if i < TILES:
-                add_residual(i, direct[0])
-            if LAG < i <= TILES:
-                rstd_of(i - LAG)
-            if i < TILES:
-                add_residual(i, direct[1])
-                for j in turned:
+                for j in direct + turned:
                     add_residual(i, j)
-            if i == LAG:
+            if i == 1:
                 quantize_x([4, 5, 6, 7], grouped47)
-            if i - 1 < TILES:
-                mean_of(i - 1)
+                for k in range(3, TILES):
+                    add_bias(k, 1, nc.gpsimd, bias_wide[:])
             if i + 1 < TILES:
-                bias_turned(i + 1, first)
                 project_turned(i + 1, second)
+                bias_turned(i + 1, second)
                 project_direct(i + 1, direct[0])
                 project_direct(i + 1, direct[1])
                 turn_back(i + 1, first)
-            if i + 2 < TILES:
-                project_turned(i + 2, first)
-            if i - 1 < TILES:
-                squares_of(i - 1)
-            if i == LAG:
-                finish_v(0, 0)
-            shift_of(i - LAG)
-            if i - 1 < TILES:
-                std_of(i - 1)
-            normalise_g(i - LAG)
-            if i + 1 < TILES:
-                bias_turned(i + 1, second)
                 turn_back(i + 1, second)
-            if i > LAG:
-                finish_v(i - LAG, TILES - 1 if i == TILES else None)
-            finish_g(i - LAG)
+            if i == 1:
+                gain_head = fixed.tile([P, BANK_BF16], BF16, name="gain_head", tag="f2")
+                spread(gain_head, norm_rows, 0, 0, BANK_BF16)
+                both_tail = fixed.tile([P, 2 * tail], BF16, name="both_tail", tag="f0")
+                spread(both_tail[:, 0:tail], norm_rows, 0, BANK_BF16, V_MAX)
+            if i <= TILES:
+                squares_of(i - 1)
+                small = [lambda: rstd_of(i - 1), lambda: shift_of(i - 1)]
+                if i < TILES:
+                    small = [small[0], lambda: mean_of(i), small[1]]
+                if i + 2 < TILES:
+                    project_turned(i + 2, first)
+                    bias_turned(i + 2, first, small)
+                else:
+                    for step in small:
+                        step()
+                normalise_g(i - 1)
+            if i == 1:
+                beta_head = fixed.tile([P, BANK_BF16], BF16, name="beta_head", tag="f1")
+                spread(beta_head, norm_rows, BLOCKS, 0, BANK_BF16)
+                spread(both_tail[:, tail : 2 * tail], norm_rows, BLOCKS, BANK_BF16, V_MAX)
+            if i >= LAG:
+                finish_v(i - LAG)
+            if i <= TILES:
+                finish_g(i - 1)
             if i >= LAG + STORE_LAG:
                 store_g(i - LAG - STORE_LAG)
         for i in range(TILES - STORE_LAG, TILES):

@@ -26,20 +26,20 @@ SUBS = BLOCK // P
 TILES = LQ // P
 BANK_BF16 = 1024
 HALF = D // 2
-TURNED = 2
+TURNED = [2,2,2,2,2,2,2,2]
 V_MAX = 1536
-G_MIN = 1024
-V_COLS = [1376,1376,1376,1376,1376,1376,1376,1376]
+G_MIN = 1344
+V_COLS = [1344,1344,1344,1344,1344,1344,1344,1536]
 LAG = 2
-STORE_LAG = 0
+WOVEN = 6
 
 
 def tile_multiheadattention_pb_kernel(
     tc, attn_out, residual, proj_w_words, proj_w_scales, proj_b, ln_g, ln_b, out
 ):
     nc = tc.nc
-    turned = list(range(TURNED))
-    direct = list(range(TURNED, BLOCKS))
+    turned = [list(range(n)) for n in TURNED]
+    direct = [list(range(n, BLOCKS)) for n in TURNED]
     tail = V_MAX - BANK_BF16
 
     with ExitStack() as ctx:
@@ -81,8 +81,6 @@ def tile_multiheadattention_pb_kernel(
         beta_g = keep.tile([P, D - G_MIN], BF16)
         load_x(0)
         load_x(1)
-        load_x(2)
-        load_x(3)
         nc.sync.dma_start(out=bias_rows[0:BLOCKS, :], in_=proj_b.rearrange("(r n) -> r n", n=BLOCK))
         for q in range(4):
             nc.sync.dma_start(
@@ -91,6 +89,8 @@ def tile_multiheadattention_pb_kernel(
             )
         nc.sync.dma_start(out=w_words[:].bitcast(I32), in_=proj_w_words[0].bitcast(I32))
         load_res(0)
+        load_x(2)
+        load_x(3)
         load_res(1)
         load_x(4)
         load_x(5)
@@ -101,11 +101,11 @@ def tile_multiheadattention_pb_kernel(
         nc.sync.dma_start(out=norm_rows[BLOCKS : 2 * BLOCKS, :], in_=ln_b.rearrange("(r n) -> r n", n=BLOCK))
         load_res(3)
         load_res(4)
-        nc.sync.dma_start(out=gain_g[:], in_=ln_g[G_MIN:D].partition_broadcast(P))
-        nc.sync.dma_start(out=beta_g[:], in_=ln_b[G_MIN:D].partition_broadcast(P))
         load_res(5)
         load_res(6)
         load_res(7)
+        nc.sync.dma_start(out=gain_g[:], in_=ln_g[G_MIN:D].partition_broadcast(P))
+        nc.sync.dma_start(out=beta_g[:], in_=ln_b[G_MIN:D].partition_broadcast(P))
 
         x_codes = {}
         x_scales = {}
@@ -147,11 +147,10 @@ def tile_multiheadattention_pb_kernel(
 
         res_bias = {}
 
-        def add_bias(i, half, engine, bias):
-            res_bias[i, half] = keep.tile([P, HALF], F32, name="res_bias", tag="res_bias%d" % i, align_bytes=64)
-            engine.tensor_tensor(
-                out=res_bias[i, half][:], in0=res[i][:, half * HALF : (half + 1) * HALF], in1=bias, op=ALU.add
-            )
+        def add_bias(i, engine, bias):
+            c0 = TURNED[i] * BLOCK
+            res_bias[i] = keep.tile([P, D - c0], F32, name="res_bias", tag="res_bias%d" % i, align_bytes=64)
+            engine.tensor_tensor(out=res_bias[i][:], in0=res[i][:, c0:D], in1=bias[:, c0 - HALF : HALF], op=ALU.add)
 
         proj = {}
         turned_sb = {}
@@ -216,8 +215,8 @@ def tile_multiheadattention_pb_kernel(
                 y[i] = work.tile([P, D], F32, name="y", bufs=4)
                 sums[i] = stat.tile([P, BLOCKS], F32, name="sums")
             cols = slice(j * BLOCK, (j + 1) * BLOCK)
-            half, at = divmod(j * BLOCK, HALF)
-            other = res_bias[i, half][:, at : at + BLOCK] if (i, half) in res_bias else res[i][:, cols]
+            at = (j - TURNED[i]) * BLOCK
+            other = res_bias[i][:, at : at + BLOCK] if j in direct[i] else res[i][:, cols]
             nc.vector.scalar_tensor_tensor(
                 out=y[i][:, cols],
                 in0=proj[i, j][:],
@@ -258,17 +257,25 @@ def tile_multiheadattention_pb_kernel(
                 out=out_g[i][:], in_=y[i][:, V_COLS[i] : D], func=ACT.Identity, scale=rstd[i][:], bias=shift[i][:]
             )
 
-        def finish_g(i):
+        def gain_g_of(i):
             cols = slice(V_COLS[i] - G_MIN, D - G_MIN)
             nc.gpsimd.tensor_tensor(out=out_g[i][:], in0=out_g[i][:], in1=gain_g[:, cols], op=ALU.mult)
+
+        def beta_g_of(i):
+            cols = slice(V_COLS[i] - G_MIN, D - G_MIN)
             nc.gpsimd.tensor_tensor(out=out_g[i][:], in0=out_g[i][:], in1=beta_g[:, cols], op=ALU.add)
 
         def store_g(i):
-            nc.sync.dma_start(out=out[i * P : (i + 1) * P, V_COLS[i] : D], in_=out_g[i][:])
+            queue = nc.scalar if i == TILES - 1 else nc.sync
+            queue.dma_start(out=out[i * P : (i + 1) * P, V_COLS[i] : D], in_=out_g[i][:])
 
         def finish_v(i):
-            out_v = work.tile([P, V_COLS[i]], F32, name="out_v")
-            parts = [(slice(0, BANK_BF16), gain_head[:], beta_head[:])]
+            out_v = work.tile([P, V_COLS[i]], F32, name="out_v", bufs=4)
+            width = BLOCK if i == TILES - 1 else BANK_BF16
+            parts = [
+                (slice(c, c + width), gain_head[:, c : c + width], beta_head[:, c : c + width])
+                for c in range(0, BANK_BF16, width)
+            ]
             rest = V_COLS[i] - BANK_BF16
             if rest:
                 parts.append((slice(BANK_BF16, V_COLS[i]), both_tail[:, 0:rest], both_tail[:, tail : tail + rest]))
@@ -282,12 +289,11 @@ def tile_multiheadattention_pb_kernel(
                 )
                 nc.sync.dma_start(out=out[i * P : (i + 1) * P, cols], in_=out_v[:, cols])
 
-        first, second = turned
-        grouped03 = keep.tile([P, 4 * HV], BF16, align_bytes=64)
+        grouped01 = keep.tile([P, 2 * HV], BF16, align_bytes=64)
+        grouped23 = keep.tile([P, 2 * HV], BF16, name="grouped23", tag="res_bias1", align_bytes=64)
         grouped47 = keep.tile([P, 4 * HV], BF16, name="grouped47", tag="res_bias3", align_bytes=64)
-        turn_x([0, 1], grouped03, 0, "f0")
-        turn_x([2, 3], grouped03, 2, "f1")
-        quantize_x([0, 1, 2, 3], grouped03)
+        turn_x([0, 1], grouped01, 0, "f0")
+        quantize_x([0, 1], grouped01)
         bias_t = banks.tile([P, SUBS, P], BF16, name="bias_t", tag="bank")
         for s in range(SUBS):
             nc.tensor.transpose(bias_t[:, s, :], bias_rows[:, s * P : (s + 1) * P], ident_bf[:])
@@ -297,74 +303,86 @@ def tile_multiheadattention_pb_kernel(
         spread(bias_high, bias_rows, 0, HALF, D)
         bias_wide = keep.tile([P, HALF], BF16)
         nc.scalar.copy(out=bias_wide[:], in_=bias_high[:])
-        add_bias(0, 1, nc.vector, bias_high[:])
-        add_bias(1, 1, nc.gpsimd, bias_wide[:])
 
-        for j in turned:
+        for j in turned[0]:
             project_turned(0, j)
             bias_turned(0, j)
-        for j in direct:
+        for j in direct[0]:
             project_direct(0, j)
-        project_turned(1, first)
-        bias_turned(1, first)
-        for j in turned:
-            turn_back(0, j)
-        for j in direct + turned:
+        turn_x([2, 3], grouped23, 0, "f1")
+        project_turned(1, 0)
+        bias_turned(1, 0)
+        add_bias(0, nc.vector, bias_high)
+        for j in direct[0]:
             add_residual(0, j)
-        project_turned(1, second)
-        bias_turned(1, second)
+        quantize_x([2, 3], grouped23)
+        add_bias(1, nc.gpsimd, bias_wide)
+        for j in turned[0]:
+            turn_back(0, j)
+        for j in turned[0]:
+            add_residual(0, j)
+        project_turned(1, 1)
+        bias_turned(1, 1)
         turn_x([4, 5], grouped47, 0, "f0")
-        for j in direct:
+        for j in direct[1]:
             project_direct(1, j)
-        turn_back(1, first)
-        turn_x([6, 7], grouped47, 2, "f1")
-        turn_back(1, second)
-        add_bias(2, 1, nc.gpsimd, bias_wide[:])
-        project_turned(2, first)
+        turn_back(1, 0)
+        turn_back(1, 1)
         mean_of(0)
-        bias_turned(2, first)
+        squares_of(0)
+        turn_x([6, 7], grouped47, 2, "f1")
+        add_bias(2, nc.gpsimd, bias_wide)
+        project_turned(2, 0)
+        bias_turned(2, 0)
 
         for i in range(1, TILES + LAG):
             if i < TILES:
-                for j in direct + turned:
+                for j in turned[i] + direct[i] if i == 1 else direct[i] + turned[i]:
                     add_residual(i, j)
             if i == 1:
                 quantize_x([4, 5, 6, 7], grouped47)
                 for k in range(3, TILES):
-                    add_bias(k, 1, nc.gpsimd, bias_wide[:])
-            if i + 1 < TILES:
-                project_turned(i + 1, second)
-                bias_turned(i + 1, second)
-                project_direct(i + 1, direct[0])
-                project_direct(i + 1, direct[1])
-                turn_back(i + 1, first)
-                turn_back(i + 1, second)
-            if i == 1:
-                gain_head = fixed.tile([P, BANK_BF16], BF16, name="gain_head", tag="f2")
-                spread(gain_head, norm_rows, 0, 0, BANK_BF16)
-                both_tail = fixed.tile([P, 2 * tail], BF16, name="both_tail", tag="f0")
-                spread(both_tail[:, 0:tail], norm_rows, 0, BANK_BF16, V_MAX)
+                    add_bias(k, nc.gpsimd, bias_wide)
             if i <= TILES:
-                squares_of(i - 1)
                 small = [lambda: rstd_of(i - 1), lambda: shift_of(i - 1)]
-                if i < TILES:
-                    small = [small[0], lambda: mean_of(i), small[1]]
-                if i + 2 < TILES:
-                    project_turned(i + 2, first)
-                    bias_turned(i + 2, first, small)
+                if i + 1 < TILES:
+                    project_turned(i + 1, 1)
+                    bias_turned(i + 1, 1, small)
+                    for j in turned[i + 1][2:]:
+                        project_turned(i + 1, j)
+                        bias_turned(i + 1, j)
+                    for j in direct[i + 1]:
+                        project_direct(i + 1, j)
+                    if i == 1:
+                        gain_head = fixed.tile([P, BANK_BF16], BF16, name="gain_head", tag="f2")
+                        spread(gain_head, norm_rows, 0, 0, BANK_BF16)
+                        both_tail = fixed.tile([P, 2 * tail], BF16, name="both_tail", tag="f0")
+                        spread(both_tail[:, 0:tail], norm_rows, 0, BANK_BF16, V_MAX)
+                    for j in turned[i + 1]:
+                        turn_back(i + 1, j)
                 else:
                     for step in small:
                         step()
+                if i < TILES:
+                    mean_of(i)
                 normalise_g(i - 1)
+            if i < TILES:
+                squares_of(i)
+            if i + 2 < TILES:
+                project_turned(i + 2, 0)
+                bias_turned(i + 2, 0)
             if i == 1:
                 beta_head = fixed.tile([P, BANK_BF16], BF16, name="beta_head", tag="f1")
                 spread(beta_head, norm_rows, BLOCKS, 0, BANK_BF16)
                 spread(both_tail[:, tail : 2 * tail], norm_rows, BLOCKS, BANK_BF16, V_MAX)
+            if i - 1 < WOVEN:
+                gain_g_of(i - 1)
             if i >= LAG:
                 finish_v(i - LAG)
-            if i <= TILES:
-                finish_g(i - 1)
-            if i >= LAG + STORE_LAG:
-                store_g(i - LAG - STORE_LAG)
-        for i in range(TILES - STORE_LAG, TILES):
-            store_g(i)
+                if i - LAG >= WOVEN:
+                    gain_g_of(i - LAG)
+                beta_g_of(i - LAG)
+                if 1 <= i - LAG < WOVEN:
+                    store_g(i - LAG - 1)
+                if i - LAG >= WOVEN - 1:
+                    store_g(i - LAG)

@@ -59,6 +59,9 @@ def tile_multiheadattention_pb_kernel(
         nc.vector.memset(bias_rows[:], 0.0)
         nc.vector.memset(w_scales[:].bitcast(I32), 0)
         nc.vector.memset(norm_rows[:], 0.0)
+        warm = keep.tile([P, 1], F32)
+        nc.vector.memset(warm[:], 1.0)
+        nc.scalar.activation(out=warm[:], in_=warm[:], func=ACT.Abs_reciprocal_sqrt)
         make_identity(nc, ident[:])
         make_identity(nc, ident_bf[:])
 

from contextlib import ExitStack

import concourse.mybir as mybir
from concourse.masks import make_identity

LQ, D, H, DV = 1024, 2048, 4, 128
HV = H * DV
LN_EPS = 1e-5
FLOPS = 2 * LQ * HV * D

F32 = mybir.dt.float32
BF16 = mybir.dt.bfloat16
I32 = mybir.dt.int32
U32 = mybir.dt.uint32
U8 = mybir.dt.uint8
E5M2X4 = mybir.dt.float8_e5m2_x4
E2M1X4 = mybir.dt.float4_e2m1fn_x4
ACT = mybir.ActivationFunctionType
ALU = mybir.AluOpType

P = 128
PACK = 4
BLOCK = 512
BLOCKS = D // BLOCK
SUBS = BLOCK // P
TILES = LQ // P
BANK_BF16 = 1024
HALF = D // 2
TURNED = [2,2,2,2,2,2,2,2]
V_MAX = 1536
G_MIN = 1344
V_COLS = [1344,1344,1344,1344,1344,1344,1344,1536]
LAG = 2
WOVEN = 6


def tile_multiheadattention_pb_kernel(
    tc, attn_out, residual, proj_w_words, proj_w_scales, proj_b, ln_g, ln_b, out
):
    nc = tc.nc
    turned = [list(range(n)) for n in TURNED]
    direct = [list(range(n, BLOCKS)) for n in TURNED]
    tail = V_MAX - BANK_BF16

    with ExitStack() as ctx:
        keep = ctx.enter_context(tc.tile_pool(name="keep", bufs=1))
        work = ctx.enter_context(tc.tile_pool(name="work", bufs=3))
        stat = ctx.enter_context(tc.tile_pool(name="stat", bufs=4))
        fixed = ctx.enter_context(tc.psum_pool(name="fixed", bufs=1))
        banks = ctx.enter_context(tc.psum_pool(name="banks", bufs=5))
        ctx.enter_context(tc.manual_schedule())

        bias_rows = keep.tile([P, BLOCK], BF16)
        norm_rows = keep.tile([P, BLOCK], BF16)
        w_scales = keep.tile([P, D], U8, align_bytes=64)
        w_words = keep.tile([P, 2 * D], U8, align_bytes=64)
        ident = keep.tile([P, P], F32)
        ident_bf = keep.tile([P, P], BF16)
        nc.vector.memset(bias_rows[:], 0.0)
        nc.vector.memset(w_scales[:].bitcast(I32), 0)
        nc.vector.memset(norm_rows[:], 0.0)
        warm = keep.tile([P, 1], F32)
        nc.vector.memset(warm[:], 1.0)
        nc.scalar.activation(out=warm[:], in_=warm[:], func=ACT.Abs_reciprocal_sqrt)
        make_identity(nc, ident[:])
        make_identity(nc, ident_bf[:])

        x_rows = []
        res = []
        for i in range(TILES):
            x_rows.append(keep.tile([P, HV], BF16, name="x_rows%d" % i))
            res.append(keep.tile([P, D], BF16, name="res%d" % i))

        def load_x(i):
            nc.sync.dma_start(
                out=x_rows[i][:].rearrange("p (h j) -> p h j", h=H),
                in_=attn_out[:, i * P : (i + 1) * P, :].rearrange("h p j -> p h j"),
            )

        def load_res(i):
            nc.sync.dma_start(out=res[i][:], in_=residual[i * P : (i + 1) * P, :])

        gain_g = keep.tile([P, D - G_MIN], BF16)
        beta_g = keep.tile([P, D - G_MIN], BF16)
        load_x(0)
        load_x(1)
        nc.sync.dma_start(out=bias_rows[0:BLOCKS, :], in_=proj_b.rearrange("(r n) -> r n", n=BLOCK))
        for q in range(4):
            nc.sync.dma_start(
                out=w_scales[32 * q : 32 * q + 4, :].bitcast(I32),
                in_=proj_w_scales[0, 4 * q : 4 * q + 4, :].bitcast(I32),
            )
        nc.sync.dma_start(out=w_words[:].bitcast(I32), in_=proj_w_words[0].bitcast(I32))
        load_res(0)
        load_x(2)
        load_x(3)
        load_res(1)
        load_x(4)
        load_x(5)
        load_res(2)
        load_x(6)
        load_x(7)
        nc.sync.dma_start(out=norm_rows[0:BLOCKS, :], in_=ln_g.rearrange("(r n) -> r n", n=BLOCK))
        nc.sync.dma_start(out=norm_rows[BLOCKS : 2 * BLOCKS, :], in_=ln_b.rearrange("(r n) -> r n", n=BLOCK))
        load_res(3)
        load_res(4)
        load_res(5)
        load_res(6)
        load_res(7)
        nc.sync.dma_start(out=gain_g[:], in_=ln_g[G_MIN:D].partition_broadcast(P))
        nc.sync.dma_start(out=beta_g[:], in_=ln_b[G_MIN:D].partition_broadcast(P))

        x_codes = {}
        x_scales = {}

        def turn_x(tiles, grouped, first, bank):
            n = len(tiles)
            xt = fixed.tile([P, n, 2, P], F32, name="xt", tag=bank)
            for t, i in enumerate(tiles):
                words = x_rows[i][:].bitcast(F32)
                for u in range(2):
                    nc.tensor.transpose(xt[:, t, u, :], words[:, u : HV // 2 : 2], ident[:])
            nc.scalar.copy(
                out=grouped[:, first * HV : (first + n) * HV].bitcast(F32).rearrange("p (t r u) -> p t r u", t=n, u=2),
                in_=xt[:].rearrange("p t u r -> p t r u"),
            )

        def quantize_x(tiles, grouped):
            n = len(tiles)
            codes = keep.tile([P, n * P], U32, name="codes%d" % tiles[0], align_bytes=64)
            scales = keep.tile([P, n * P], U8, name="scales%d" % tiles[0], align_bytes=64)
            nc.vector.quantize_mx(out=codes[:].bitcast(E5M2X4), scales=scales[:], in_=grouped[:])
            for t, i in enumerate(tiles):
                x_codes[i] = codes[:, t * P : (t + 1) * P].bitcast(E5M2X4)
                x_scales[i] = scales[:, t * P : (t + 1) * P]

        def spread(dst, rows, first_row, c0, c1):
            c = c0
            while c < c1:
                r = c // BLOCK
                end = min(c1, (r + 1) * BLOCK, c + BLOCK - (c - c0) % BLOCK)
                nc.tensor.matmul(
                    out=dst[:, c - c0 : end - c0],
                    lhsT=ident_bf[:, first_row + r : first_row + r + 1].to_broadcast([P, P]),
                    rhs=rows[:, c - r * BLOCK : end - r * BLOCK],
                    start=True,
                    stop=True,
                )
                c = end

        res_bias = {}

        def add_bias(i, engine, bias):
            c0 = TURNED[i] * BLOCK
            res_bias[i] = keep.tile([P, D - c0], F32, name="res_bias", tag="res_bias%d" % i, align_bytes=64)
            engine.tensor_tensor(out=res_bias[i][:], in0=res[i][:, c0:D], in1=bias[:, c0 - HALF : HALF], op=ALU.add)

        proj = {}
        turned_sb = {}

        def project_turned(i, j):
            acc = banks.tile([P, BLOCK], F32, name="acc", tag="bank")
            for s in range(SUBS):
                c0 = j * BLOCK + s * P
                nc.tensor.matmul_mx(
                    out=acc[:, s * P : (s + 1) * P],
                    lhsT=w_words[:, 2 * c0 : 2 * (c0 + P)].bitcast(E2M1X4),
                    lhsT_scale=w_scales[:, c0 : c0 + P],
                    rhs=x_codes[i],
                    rhs_scale=x_scales[i],
                    start=True,
                    stop=True,
                )
            proj[i, j] = acc

        def bias_turned(i, j, between=()):
            sb = work.tile([P, BLOCK], F32, name="turned%d" % j)
            turned_sb[i, j] = sb
            for s in range(SUBS):
                nc.scalar.activation(
                    out=sb[:, s * P : (s + 1) * P],
                    in_=proj[i, j][:, s * P : (s + 1) * P],
                    func=ACT.Identity,
                    bias=bias_cols[:, s, j : j + 1],
                )
                if s < len(between):
                    between[s]()

        def turn_back(i, j):
            for s in range(SUBS):
                nc.tensor.transpose(
                    proj[i, j][:, s * P : (s + 1) * P], turned_sb[i, j][:, s * P : (s + 1) * P], ident[:]
                )

        def project_direct(i, j):
            acc = banks.tile([P, BLOCK], F32, name="acc", tag="bank")
            nc.tensor.matmul_mx(
                out=acc[:],
                lhsT=x_codes[i],
                lhsT_scale=x_scales[i],
                rhs=w_words[:, 2 * j * BLOCK : 2 * (j + 1) * BLOCK].bitcast(E2M1X4),
                rhs_scale=w_scales[:, j * BLOCK : (j + 1) * BLOCK],
                start=True,
                stop=True,
            )
            proj[i, j] = acc

        y = {}
        sums = {}
        neg_mean = {}
        sum_sq = {}
        rstd = {}
        shift = {}
        out_g = {}

        def add_residual(i, j):
            if i not in y:
                y[i] = work.tile([P, D], F32, name="y", bufs=4)
                sums[i] = stat.tile([P, BLOCKS], F32, name="sums")
            cols = slice(j * BLOCK, (j + 1) * BLOCK)
            at = (j - TURNED[i]) * BLOCK
            other = res_bias[i][:, at : at + BLOCK] if j in direct[i] else res[i][:, cols]
            nc.vector.scalar_tensor_tensor(
                out=y[i][:, cols],
                in0=proj[i, j][:],
                scalar=1.0,
                in1=other,
                op0=ALU.mult,
                op1=ALU.add,
                accum_out=sums[i][:, j : j + 1],
            )

        def mean_of(i):
            scaled = stat.tile([P, BLOCKS], F32, name="scaled")
            neg_mean[i] = stat.tile([P, 1], F32, name="neg_mean")
            nc.scalar.activation(
                out=scaled[:], in_=sums[i][:], func=ACT.Identity, scale=-1.0 / D, accum_out=neg_mean[i][:]
            )

        def squares_of(i):
            squares = keep.tile([P, D], BF16, name="squares")
            sum_sq[i] = stat.tile([P, 1], F32, name="sum_sq")
            nc.scalar.activation(
                out=squares[:], in_=y[i][:], func=ACT.Square, bias=neg_mean[i][:], accum_out=sum_sq[i][:]
            )

        def rstd_of(i):
            rstd[i] = stat.tile([P, 1], F32, name="rstd")
            nc.scalar.activation(
                out=rstd[i][:], in_=sum_sq[i][:], func=ACT.Abs_reciprocal_sqrt, scale=1.0 / D, bias=LN_EPS
            )

        def shift_of(i):
            shift[i] = stat.tile([P, 1], F32, name="shift")
            nc.scalar.activation(out=shift[i][:], in_=neg_mean[i][:], func=ACT.Identity, scale=rstd[i][:])

        def normalise_g(i):
            out_g[i] = work.tile([P, D - V_COLS[i]], F32, name="out_g", bufs=5)
            nc.scalar.activation(
                out=out_g[i][:], in_=y[i][:, V_COLS[i] : D], func=ACT.Identity, scale=rstd[i][:], bias=shift[i][:]
            )

        def gain_g_of(i):
            cols = slice(V_COLS[i] - G_MIN, D - G_MIN)
            nc.gpsimd.tensor_tensor(out=out_g[i][:], in0=out_g[i][:], in1=gain_g[:, cols], op=ALU.mult)

        def beta_g_of(i):
            cols = slice(V_COLS[i] - G_MIN, D - G_MIN)
            nc.gpsimd.tensor_tensor(out=out_g[i][:], in0=out_g[i][:], in1=beta_g[:, cols], op=ALU.add)

        def store_g(i):
            queue = nc.scalar if i == TILES - 1 else nc.sync
            queue.dma_start(out=out[i * P : (i + 1) * P, V_COLS[i] : D], in_=out_g[i][:])

        def finish_v(i):
            out_v = work.tile([P, V_COLS[i]], F32, name="out_v", bufs=4)
            width = BLOCK if i == TILES - 1 else BANK_BF16
            parts = [
                (slice(c, c + width), gain_head[:, c : c + width], beta_head[:, c : c + width])
                for c in range(0, BANK_BF16, width)
            ]
            rest = V_COLS[i] - BANK_BF16
            if rest:
                parts.append((slice(BANK_BF16, V_COLS[i]), both_tail[:, 0:rest], both_tail[:, tail : tail + rest]))
            for cols, gain, beta in parts:
                nc.vector.scalar_tensor_tensor(
                    out=out_v[:, cols], in0=y[i][:, cols], scalar=neg_mean[i][:], in1=gain, op0=ALU.add, op1=ALU.mult
                )
            for cols, gain, beta in parts:
                nc.vector.scalar_tensor_tensor(
                    out=out_v[:, cols], in0=out_v[:, cols], scalar=rstd[i][:], in1=beta, op0=ALU.mult, op1=ALU.add
                )
                nc.sync.dma_start(out=out[i * P : (i + 1) * P, cols], in_=out_v[:, cols])

        grouped01 = keep.tile([P, 2 * HV], BF16, align_bytes=64)
        grouped23 = keep.tile([P, 2 * HV], BF16, name="grouped23", tag="res_bias1", align_bytes=64)
        grouped47 = keep.tile([P, 4 * HV], BF16, name="grouped47", tag="res_bias3", align_bytes=64)
        turn_x([0, 1], grouped01, 0, "f0")
        quantize_x([0, 1], grouped01)
        bias_t = banks.tile([P, SUBS, P], BF16, name="bias_t", tag="bank")
        for s in range(SUBS):
            nc.tensor.transpose(bias_t[:, s, :], bias_rows[:, s * P : (s + 1) * P], ident_bf[:])
        bias_cols = keep.tile([P, SUBS, BLOCKS], F32)
        nc.scalar.copy(out=bias_cols[:], in_=bias_t[:, :, 0:BLOCKS])
        bias_high = fixed.tile([P, HALF], BF16, name="bias_high", tag="f2")
        spread(bias_high, bias_rows, 0, HALF, D)
        bias_wide = keep.tile([P, HALF], BF16)
        nc.scalar.copy(out=bias_wide[:], in_=bias_high[:])

        for j in turned[0]:
            project_turned(0, j)
            bias_turned(0, j)
        for j in direct[0]:
            project_direct(0, j)
        turn_x([2, 3], grouped23, 0, "f1")
        project_turned(1, 0)
        bias_turned(1, 0)
        add_bias(0, nc.vector, bias_high)
        for j in direct[0]:
            add_residual(0, j)
        quantize_x([2, 3], grouped23)
        add_bias(1, nc.gpsimd, bias_wide)
        for j in turned[0]:
            turn_back(0, j)
        for j in turned[0]:
            add_residual(0, j)
        project_turned(1, 1)
        bias_turned(1, 1)
        turn_x([4, 5], grouped47, 0, "f0")
        for j in direct[1]:
            project_direct(1, j)
        turn_back(1, 0)
        turn_back(1, 1)
        mean_of(0)
        squares_of(0)
        turn_x([6, 7], grouped47, 2, "f1")
        add_bias(2, nc.gpsimd, bias_wide)
        project_turned(2, 0)
        bias_turned(2, 0)

        for i in range(1, TILES + LAG):
            if i < TILES:
                for j in turned[i] + direct[i] if i == 1 else direct[i] + turned[i]:
                    add_residual(i, j)
            if i == 1:
                quantize_x([4, 5, 6, 7], grouped47)
                for k in range(3, TILES):
                    add_bias(k, nc.gpsimd, bias_wide)
            if i <= TILES:
                small = [lambda: rstd_of(i - 1), lambda: shift_of(i - 1)]
                if i + 1 < TILES:
                    project_turned(i + 1, 1)
                    bias_turned(i + 1, 1, small)
                    for j in turned[i + 1][2:]:
                        project_turned(i + 1, j)
                        bias_turned(i + 1, j)
                    for j in direct[i + 1]:
                        project_direct(i + 1, j)
                    if i == 1:
                        gain_head = fixed.tile([P, BANK_BF16], BF16, name="gain_head", tag="f2")
                        spread(gain_head, norm_rows, 0, 0, BANK_BF16)
                        both_tail = fixed.tile([P, 2 * tail], BF16, name="both_tail", tag="f0")
                        spread(both_tail[:, 0:tail], norm_rows, 0, BANK_BF16, V_MAX)
                    for j in turned[i + 1]:
                        turn_back(i + 1, j)
                else:
                    for step in small:
                        step()
                if i < TILES:
                    mean_of(i)
                normalise_g(i - 1)
            if i < TILES:
                squares_of(i)
            if i + 2 < TILES:
                project_turned(i + 2, 0)
                bias_turned(i + 2, 0)
            if i == 1:
                beta_head = fixed.tile([P, BANK_BF16], BF16, name="beta_head", tag="f1")
                spread(beta_head, norm_rows, BLOCKS, 0, BANK_BF16)
                spread(both_tail[:, tail : 2 * tail], norm_rows, BLOCKS, BANK_BF16, V_MAX)
            if i - 1 < WOVEN:
                gain_g_of(i - 1)
            if i >= LAG:
                finish_v(i - LAG)
                if i - LAG >= WOVEN:
                    gain_g_of(i - LAG)
                beta_g_of(i - LAG)
                if 1 <= i - LAG < WOVEN:
                    store_g(i - LAG - 1)
                if i - LAG >= WOVEN - 1:
                    store_g(i - LAG)
